import numpy as np
import ml_dtypes


def mxq(x, axis, fmt="e4m3"):
    dtype, down = {"e4m3": (ml_dtypes.float8_e4m3fn, 7), "e5m2": (ml_dtypes.float8_e5m2, 14)}[fmt]
    v = np.moveaxis(np.asarray(x, np.float32).astype(ml_dtypes.bfloat16).astype(np.float64), axis, -1)
    blocks = v.reshape(v.shape[:-1] + (-1, 32))
    amax = np.abs(blocks).max(-1, keepdims=True)
    byte = np.maximum(np.where(amax > 0, np.frexp(amax)[1] - 1 + 127, 0) - down, 1)
    scale = np.exp2(byte - 127.0)
    codes = (blocks / scale).astype(np.float32).astype(dtype).astype(np.float64)
    return np.moveaxis((codes * scale).reshape(v.shape), -1, axis)


WIDE = False


def mx_kscale(k):
    if not WIDE:
        return np.ones(k)
    levels = np.array([10, -10, 5, -5, 0])
    a = np.random.permutation(np.resize(levels, k // 512 * 4)).reshape(k // 512, 4)
    idx = np.arange(k)
    return np.exp2(a[idx // 512, idx % 128 // 32])


BF16 = ml_dtypes.bfloat16


def bf(x):
    return np.asarray(x, np.float32).astype(BF16)


def f64(x):
    return np.asarray(x).astype(np.float64)


B, T, D = 4, 1024, 512
G = 0.78 * D ** 0.25


def setup_inputs():
    s = mx_kscale(D)
    n = np.random.standard_normal((B, T, D))
    n = n - n.mean(axis=1, keepdims=True)
    off = np.random.standard_normal((B, 1, D))
    y = G * n * s + off * np.minimum(s, 1.0)
    w = np.random.standard_normal((B, T, D))
    y_obs = np.random.standard_normal((B, T, D)) * 1.5
    return {"x": bf(np.concatenate([y, w, y_obs], axis=-1)),
            "kernel": bf(np.random.standard_normal((D, D)) * G / s[:, None])}


def reference(x, kernel):
    x = f64(x)
    kernel = f64(kernel)
    d = kernel.shape[0]
    y = x[:, :, :d]
    w = x[:, :, d:2 * d]
    y_obs = x[:, :, 2 * d:3 * d]
    intensity = np.exp(w)
    e = np.exp(w - w.max(axis=2, keepdims=True))
    sm = e / e.sum(axis=2, keepdims=True)
    mean = y.mean(axis=1, keepdims=True)
    u = sm * (y - mean)
    smooth = (mxq(u, 2, "e4m3") @ mxq(kernel, 0, "e4m3")) + mean
    y_trans = y_obs - smooth
    return np.concatenate([smooth, intensity, y_trans], axis=-1)

@@ -1,0 +1,245 @@
+from contextlib import ExitStack
+
+import concourse.bass as bass
+import concourse.mybir as mybir
+import concourse.tile as tile
+from concourse.masks import make_identity
+
+FP8X4 = mybir.dt.float8_e4m3fn_x4
+BF16 = mybir.dt.bfloat16
+F32 = mybir.dt.float32
+U32 = mybir.dt.uint32
+U8 = mybir.dt.uint8
+ALU = mybir.AluOpType
+ACT = mybir.ActivationFunctionType
+AX = mybir.AxisListType
+
+NB, T, D = 4, 1024, 512
+P = 128
+J = T // P
+KT = D // P
+NPAIR = NB * J // 2
+ONES_N = 32
+
+FLOPS = 2 * NB * T * D * D
+
+
+def tile_crosschannelinterp_t_kernel(tc, x, kernel, out):
+    nc = tc.nc
+    with ExitStack() as ctx:
+        const = ctx.enter_context(tc.tile_pool(name="const", bufs=1))
+        xpool = ctx.enter_context(tc.tile_pool(name="xpool", bufs=1))
+        opool = ctx.enter_context(tc.tile_pool(name="opool", bufs=5))
+        epool = ctx.enter_context(tc.tile_pool(name="epool", bufs=3))
+        work = ctx.enter_context(tc.tile_pool(name="work", bufs=2))
+        stat = ctx.enter_context(tc.tile_pool(name="stat", bufs=4))
+        ps_sum = ctx.enter_context(tc.psum_pool(name="ps_sum", bufs=1))
+        ps_mean = ctx.enter_context(tc.psum_pool(name="ps_mean", bufs=2))
+        ps_xt = ctx.enter_context(tc.psum_pool(name="ps_xt", bufs=2))
+        ps_p = ctx.enter_context(tc.psum_pool(name="ps_p", bufs=3))
+
+        xv = [x[b].rearrange("(p j) c -> p j c", j=J) for b in range(NB)]
+        ov = [out[b].rearrange("(p j) c -> p j c", j=J) for b in range(NB)]
+
+        kraw = const.tile([P, KT, D], BF16, name="kraw")
+        nc.sync.dma_start(out=kraw[:], in_=kernel.rearrange("(t p) n -> p t n", p=P))
+        xb = [xpool.tile([P, J, 3 * D], BF16, name="x%d" % b) for b in range(NB)]
+        nc.sync.dma_start(out=xb[0][:, :, 0:D], in_=xv[0][:, :, 0:D])
+        nc.sync.dma_start(out=xb[0][:, 0:4, D:2 * D], in_=xv[0][:, 0:4, D:2 * D])
+        nc.sync.dma_start(out=xb[0][:, 4:8, D:2 * D], in_=xv[0][:, 4:8, D:2 * D])
+        nc.sync.dma_start(out=xb[0][:, :, 2 * D:3 * D], in_=xv[0][:, :, 2 * D:3 * D])
+        for b in range(1, NB):
+            nc.sync.dma_start(out=xb[b][:, 0:4, :], in_=xv[b][:, 0:4, :])
+            nc.sync.dma_start(out=xb[b][:, 4:8, :], in_=xv[b][:, 4:8, :])
+
+        ident_bf = const.tile([P, P], BF16, name="ident_bf")
+        make_identity(nc, ident_bf[:])
+        ident_f = const.tile([P, P], F32, name="ident_f")
+        make_identity(nc, ident_f[:])
+        ones = const.tile([P, ONES_N], BF16, name="ones")
+        nc.vector.memset(ones[:], 1.0)
+
+        kgrp = const.tile([P, D, KT], BF16, name="kgrp", align_bytes=64)
+        nc.vector.tensor_copy(out=kgrp[:], in_=kraw[:].rearrange("p t n -> p n t"))
+        kcodes = const.tile([P, D], U32, name="kcodes", align_bytes=64)
+        kscl = const.tile([P, D], U8, name="kscl", align_bytes=64)
+        nc.vector.quantize_mx(
+            out=kcodes[:].bitcast(FP8X4),
+            scales=kscl[:],
+            in_=kgrp[:].rearrange("p n t -> p (n t)"),
+        )
+
+        mean_ps = {}
+        mean_sb = {}
+        negmax = {}
+        e_t = {}
+        rs_t = {}
+        u_t = {}
+        xt_t = {}
+        ob_t = {}
+        pp_t = {}
+        d_t = {}
+        grp_t = {}
+
+        msum_t = {}
+        rep_t = {}
+        ssum_t = {}
+
+        def mean_mm(b):
+            msum = ps_sum.tile([P, KT, ONES_N], F32, name="msum")
+            for c in range(KT):
+                for j in range(J):
+                    nc.tensor.matmul(
+                        out=msum[:, c, :],
+                        lhsT=xb[b][:, j, c * P:(c + 1) * P],
+                        rhs=ones[:],
+                        start=(j == 0),
+                        stop=(j == J - 1),
+                    )
+            msum_t[b] = msum
+
+        def mean_rep(b):
+            rep = work.tile([P, KT, P], F32, name="rep")
+            nc.vector.tensor_scalar(
+                out=rep[:],
+                in0=msum_t[b][:, :, 0:1].to_broadcast([P, KT, P]),
+                scalar1=1.0 / T,
+                scalar2=None,
+                op0=ALU.mult,
+            )
+            rep_t[b] = rep
+
+        def mean_tr(b):
+            mps = ps_mean.tile([P, D], F32, name="mps")
+            for c in range(KT):
+                nc.tensor.transpose(mps[:, c * P:(c + 1) * P], rep_t[b][:, c, :], ident_f[:])
+            mean_ps[b] = mps
+
+        def mean_copy(b):
+            msb = work.tile([P, D], F32, name="msb")
+            nc.scalar.copy(out=msb[:], in_=mean_ps[b][:])
+            mean_sb[b] = msb
+
+        def rowmax(h):
+            b, j0 = h // 2, 4 * (h % 2)
+            t1 = work.tile([P, 4, 256], BF16, name="t1")
+            nc.vector.tensor_tensor(out=t1[:], in0=xb[b][:, j0:j0 + 4, D:D + 256],
+                                    in1=xb[b][:, j0:j0 + 4, D + 256:2 * D], op=ALU.max)
+            t2 = work.tile([P, 4, 128], BF16, name="t2")
+            nc.vector.tensor_tensor(out=t2[:], in0=t1[:, :, 0:128], in1=t1[:, :, 128:256], op=ALU.max)
+            t3 = work.tile([P, 4, 64], BF16, name="t3")
+            nc.vector.tensor_tensor(out=t3[:], in0=t2[:, :, 0:64], in1=t2[:, :, 64:128], op=ALU.max)
+            t4 = work.tile([P, 4, 32], BF16, name="t4")
+            nc.vector.tensor_tensor(out=t4[:], in0=t3[:, :, 0:32], in1=t3[:, :, 32:64], op=ALU.max)
+            nm = stat.tile([P, 4], F32, name="nm")
+            nc.vector.tensor_reduce(out=nm[:], in_=t4[:], axis=AX.X, op=ALU.max, negate=True)
+            negmax[h] = nm
+
+        def expo(q, a):
+            b, j0 = q // 4, 2 * (q % 4)
+            if a == 0:
+                e_t[q] = epool.tile([P, 2, D], F32, name="e")
+                ssum_t[q] = stat.tile([P, 2], F32, name="ssum")
+            col = 2 * (q % 2) + a
+            nc.scalar.activation(
+                out=e_t[q][:, a, :], in_=xb[b][:, j0 + a, D:2 * D], func=ACT.Exp,
+                bias=negmax[q // 2][:, col:col + 1], scale=1.0, accum_out=ssum_t[q][:, a:a + 1],
+            )
+
+        def centre(q):
+            b, j0 = q // 4, 2 * (q % 4)
+            d = work.tile([P, 2, D], F32, name="d")
+            nc.vector.tensor_tensor(
+                out=d[:], in0=xb[b][:, j0:j0 + 2, 0:D],
+                in1=mean_ps[b][:].unsqueeze(1).to_broadcast([P, 2, D]), op=ALU.subtract,
+            )
+            d_t[q] = d
+
+        def weigh(q):
+            rs = stat.tile([P, 2], F32, name="rs")
+            nc.vector.reciprocal(out=rs[:], in_=ssum_t[q][:])
+            u = work.tile([P, 2, D], BF16, name="u")
+            for a in range(2):
+                nc.vector.scalar_tensor_tensor(
+                    out=u[:, a, :], in0=d_t[q][:, a, :], scalar=rs[:, a:a + 1], in1=e_t[q][:, a, :],
+                    op0=ALU.mult, op1=ALU.mult,
+                )
+            xt = ps_xt.tile([P, 2, KT, P], BF16, name="xt")
+            for a in range(2):
+                for t in range(KT):
+                    nc.tensor.transpose(xt[:, a, t, :], u[:, a, t * P:(t + 1) * P], ident_bf[:])
+            xt_t[q] = xt
+
+        def regroup(q):
+            grp = work.tile([P, 2, P, KT], BF16, name="grp", align_bytes=64)
+            nc.scalar.copy(out=grp[:], in_=xt_t[q][:].rearrange("p a t r -> p a r t"))
+            grp_t[q] = grp
+
+        def quant(q):
+            codes = work.tile([P, 2 * P], U32, name="codes", align_bytes=64)
+            scl = work.tile([P, 2 * P], U8, name="scl", align_bytes=64)
+            nc.vector.quantize_mx(
+                out=codes[:].bitcast(FP8X4), scales=scl[:],
+                in_=grp_t[q][:].rearrange("p a r t -> p (a r t)"),
+            )
+            pps = []
+            for a in range(2):
+                pp = ps_p.tile([P, D], F32, name="pp")
+                nc.tensor.matmul_mx(
+                    out=pp[:],
+                    lhsT=codes[:, a * P:(a + 1) * P].bitcast(FP8X4),
+                    lhsT_scale=scl[:, a * P:(a + 1) * P],
+                    rhs=kcodes[:].bitcast(FP8X4),
+                    rhs_scale=kscl[:],
+                    start=True, stop=True,
+                )
+                pps.append(pp)
+            pp_t[q] = pps
+
+        def intensity(q):
+            b, j0 = q // 4, 2 * (q % 4)
+            ob = opool.tile([P, 2, 3 * D], F32, name="ob")
+            nc.scalar.activation(out=ob[:, :, D:2 * D], in_=xb[b][:, j0:j0 + 2, D:2 * D], func=ACT.Exp)
+            ob_t[q] = ob
+
+        def post(q):
+            b, j0 = q // 4, 2 * (q % 4)
+            ob = ob_t[q]
+            for a in range(2):
+                nc.vector.tensor_tensor(out=ob[:, a, 0:D], in0=pp_t[q][a][:], in1=mean_sb[b][:], op=ALU.add)
+            nc.gpsimd.tensor_tensor(out=ob[:, :, 2 * D:3 * D], in0=xb[b][:, j0:j0 + 2, 2 * D:3 * D],
+                                    in1=ob[:, :, 0:D], op=ALU.subtract)
+            nc.sync.dma_start(out=ov[b][:, j0:j0 + 2, :], in_=ob[:])
+
+        mean_mm(0)
+        mean_rep(0)
+        mean_tr(0)
+        rowmax(0)
+        expo(0, 0)
+        expo(0, 1)
+        mean_copy(0)
+        for s in range(NPAIR + 2):
+            nxt = s // 4 + 1
+            if 0 <= s - 2 < NPAIR:
+                post(s - 2)
+            if s % 4 == 2 and nxt < NB:
+                mean_rep(nxt)
+                mean_tr(nxt)
+            if s + 1 < NPAIR:
+                expo(s + 1, 0)
+            if s + 2 < NPAIR and s % 2 == 0:
+                rowmax((s + 2) // 2)
+            if s < NPAIR:
+                centre(s)
+            if 0 <= s - 1 < NPAIR:
+                regroup(s - 1)
+                quant(s - 1)
+                intensity(s - 1)
+            if s + 1 < NPAIR:
+                expo(s + 1, 1)
+            if s % 4 == 2 and nxt < NB:
+                mean_copy(nxt)
+            if s < NPAIR:
+                weigh(s)
+            if s % 4 == 1 and nxt < NB:
+                mean_mm(nxt)

@@ -207,7 +207,7 @@ def tile_crosschannelinterp_t_kernel(tc, x, kernel, out):
             ob = ob_t[q]
             for a in range(2):
                 nc.vector.tensor_tensor(out=ob[:, a, 0:D], in0=pp_t[q][a][:], in1=mean_sb[b][:], op=ALU.add)
-            nc.gpsimd.tensor_tensor(out=ob[:, :, 2 * D:3 * D], in0=xb[b][:, j0:j0 + 2, 2 * D:3 * D],
+            nc.vector.tensor_tensor(out=ob[:, :, 2 * D:3 * D], in0=xb[b][:, j0:j0 + 2, 2 * D:3 * D],
                                     in1=ob[:, :, 0:D], op=ALU.subtract)
             nc.sync.dma_start(out=ov[b][:, j0:j0 + 2, :], in_=ob[:])
 

@@ -1,8 +1,6 @@
 from contextlib import ExitStack
 
-import concourse.bass as bass
 import concourse.mybir as mybir
-import concourse.tile as tile
 from concourse.masks import make_identity
 
 FP8X4 = mybir.dt.float8_e4m3fn_x4
@@ -19,9 +17,14 @@ P = 128
 J = T // P
 KT = D // P
 NPAIR = NB * J // 2
+NQUAD = NB * J // 4
 ONES_N = 32
 
 FLOPS = 2 * NB * T * D * D
+
+
+def norm_on_vector(q, a):
+    return a == 0 and q % 2 == 0
 
 
 def tile_crosschannelinterp_t_kernel(tc, x, kernel, out):
@@ -33,16 +36,19 @@ def tile_crosschannelinterp_t_kernel(tc, x, kernel, out):
         epool = ctx.enter_context(tc.tile_pool(name="epool", bufs=3))
         work = ctx.enter_context(tc.tile_pool(name="work", bufs=2))
         stat = ctx.enter_context(tc.tile_pool(name="stat", bufs=4))
-        ps_sum = ctx.enter_context(tc.psum_pool(name="ps_sum", bufs=1))
-        ps_mean = ctx.enter_context(tc.psum_pool(name="ps_mean", bufs=2))
-        ps_xt = ctx.enter_context(tc.psum_pool(name="ps_xt", bufs=2))
-        ps_p = ctx.enter_context(tc.psum_pool(name="ps_p", bufs=3))
+        ps_mean = ctx.enter_context(tc.psum_pool(name="ps_mean", bufs=1))
+        ps_yt = ctx.enter_context(tc.psum_pool(name="ps_yt", bufs=2))
+        ps_sm = ctx.enter_context(tc.psum_pool(name="ps_sm", bufs=3))
+        ps_p = ctx.enter_context(tc.psum_pool(name="ps_p", bufs=2))
 
         xv = [x[b].rearrange("(p j) c -> p j c", j=J) for b in range(NB)]
         ov = [out[b].rearrange("(p j) c -> p j c", j=J) for b in range(NB)]
 
         kraw = const.tile([P, KT, D], BF16, name="kraw")
-        nc.sync.dma_start(out=kraw[:], in_=kernel.rearrange("(t p) n -> p t n", p=P))
+        nc.sync.dma_start(
+            out=kraw[:].rearrange("q (u e) n -> q u e n", u=2),
+            in_=kernel.rearrange("(u q e) n -> q u e n", u=2, e=2),
+        )
         xb = [xpool.tile([P, J, 3 * D], BF16, name="x%d" % b) for b in range(NB)]
         nc.sync.dma_start(out=xb[0][:, :, 0:D], in_=xv[0][:, :, 0:D])
         nc.sync.dma_start(out=xb[0][:, 0:4, D:2 * D], in_=xv[0][:, 0:4, D:2 * D])
@@ -52,8 +58,6 @@ def tile_crosschannelinterp_t_kernel(tc, x, kernel, out):
             nc.sync.dma_start(out=xb[b][:, 0:4, :], in_=xv[b][:, 0:4, :])
             nc.sync.dma_start(out=xb[b][:, 4:8, :], in_=xv[b][:, 4:8, :])
 
-        ident_bf = const.tile([P, P], BF16, name="ident_bf")
-        make_identity(nc, ident_bf[:])
         ident_f = const.tile([P, P], F32, name="ident_f")
         make_identity(nc, ident_f[:])
         ones = const.tile([P, ONES_N], BF16, name="ones")
@@ -69,36 +73,39 @@ def tile_crosschannelinterp_t_kernel(tc, x, kernel, out):
             in_=kgrp[:].rearrange("p n t -> p (n t)"),
         )
 
-        mean_ps = {}
+        msum_t = {}
+        negmean = {}
         mean_sb = {}
         negmax = {}
+        yt_t = {}
+        dt_t = {}
         e_t = {}
+        ssum_t = {}
         rs_t = {}
-        u_t = {}
-        xt_t = {}
+        sm_t = {}
+        grp_t = {}
         ob_t = {}
         pp_t = {}
-        d_t = {}
-        grp_t = {}
-
-        msum_t = {}
-        rep_t = {}
-        ssum_t = {}
 
         def mean_mm(b):
-            msum = ps_sum.tile([P, KT, ONES_N], F32, name="msum")
-            for c in range(KT):
+            msum = ps_mean.tile([P, KT, ONES_N], F32, name="msum", tag="mean")
+            for t in range(KT):
                 for j in range(J):
+                    ysel = xb[b][:, j, 0:D].rearrange("p (u q e) -> p u e q", u=2, e=2)
                     nc.tensor.matmul(
-                        out=msum[:, c, :],
-                        lhsT=xb[b][:, j, c * P:(c + 1) * P],
+                        out=msum[:, t, :],
+                        lhsT=ysel[:, t // 2, t % 2, :],
                         rhs=ones[:],
                         start=(j == 0),
                         stop=(j == J - 1),
                     )
             msum_t[b] = msum
+            nm = stat.tile([P, KT, 1], F32, name="negmean")
+            nc.vector.tensor_scalar(out=nm[:], in0=msum[:, :, 0:1], scalar1=-1.0 / T, scalar2=None,
+                                    op0=ALU.mult)
+            negmean[b] = nm
 
-        def mean_rep(b):
+        def mean_bc(b):
             rep = work.tile([P, KT, P], F32, name="rep")
             nc.vector.tensor_scalar(
                 out=rep[:],
@@ -107,18 +114,37 @@ def tile_crosschannelinterp_t_kernel(tc, x, kernel, out):
                 scalar2=None,
                 op0=ALU.mult,
             )
-            rep_t[b] = rep
-
-        def mean_tr(b):
-            mps = ps_mean.tile([P, D], F32, name="mps")
-            for c in range(KT):
-                nc.tensor.transpose(mps[:, c * P:(c + 1) * P], rep_t[b][:, c, :], ident_f[:])
-            mean_ps[b] = mps
-
-        def mean_copy(b):
+            mbc = ps_mean.tile([P, KT, P], F32, name="mbc", tag="mean")
+            for t in range(KT):
+                nc.tensor.transpose(mbc[:, t, :], rep[:, t, :], ident_f[:])
             msb = work.tile([P, D], F32, name="msb")
-            nc.scalar.copy(out=msb[:], in_=mean_ps[b][:])
+            nc.scalar.copy(
+                out=msb[:].rearrange("p (u q e) -> p u q e", u=2, e=2),
+                in_=mbc[:].rearrange("p (u e) q -> p u q e", u=2),
+            )
             mean_sb[b] = msb
+
+        def ytr(h):
+            b, j0 = h // 2, 4 * (h % 2)
+            xw = xb[b][:].bitcast(F32)
+            yts = []
+            for u in range(2):
+                yt = ps_yt.tile([P, 4 * P], F32, name="yt")
+                for a4 in range(4):
+                    nc.tensor.transpose(yt[:, a4 * P:(a4 + 1) * P], xw[:, j0 + a4, u * P:(u + 1) * P],
+                                        ident_f[:])
+                yts.append(yt)
+            yt_t[h] = yts
+
+        def centre(h, u):
+            b = h // 2
+            if u == 0:
+                dt_t[h] = work.tile([P, KT, 4 * P], F32, name="dT")
+            pairs = yt_t[h][u][:].bitcast(BF16).rearrange("p (r e) -> p r e", e=2)
+            for e in range(2):
+                t = 2 * u + e
+                nc.scalar.activation(out=dt_t[h][:, t, :], in_=pairs[:, :, e], func=ACT.Identity,
+                                     bias=negmean[b][:, t, :], scale=1.0)
 
         def rowmax(h):
             b, j0 = h // 2, 4 * (h % 2)
@@ -135,44 +161,50 @@ def tile_crosschannelinterp_t_kernel(tc, x, kernel, out):
             nc.vector.tensor_reduce(out=nm[:], in_=t4[:], axis=AX.X, op=ALU.max, negate=True)
             negmax[h] = nm
 
-        def expo(q, a):
+        def expo(q):
             b, j0 = q // 4, 2 * (q % 4)
-            if a == 0:
-                e_t[q] = epool.tile([P, 2, D], F32, name="e")
-                ssum_t[q] = stat.tile([P, 2], F32, name="ssum")
-            col = 2 * (q % 2) + a
-            nc.scalar.activation(
-                out=e_t[q][:, a, :], in_=xb[b][:, j0 + a, D:2 * D], func=ACT.Exp,
-                bias=negmax[q // 2][:, col:col + 1], scale=1.0, accum_out=ssum_t[q][:, a:a + 1],
-            )
+            e_t[q] = epool.tile([P, 2, D], F32, name="e")
+            ssum_t[q] = stat.tile([P, 2], F32, name="ssum")
+            for a in range(2):
+                col = 2 * (q % 2) + a
+                nc.scalar.activation(
+                    out=e_t[q][:, a, :].rearrange("p (u e q) -> p u e q", u=2, e=2),
+                    in_=xb[b][:, j0 + a, D:2 * D].rearrange("p (u q e) -> p u e q", u=2, e=2),
+                    func=ACT.Exp,
+                    bias=negmax[q // 2][:, col:col + 1], scale=1.0, accum_out=ssum_t[q][:, a:a + 1],
+                )
 
-        def centre(q):
-            b, j0 = q // 4, 2 * (q % 4)
-            d = work.tile([P, 2, D], F32, name="d")
-            nc.vector.tensor_tensor(
-                out=d[:], in0=xb[b][:, j0:j0 + 2, 0:D],
-                in1=mean_ps[b][:].unsqueeze(1).to_broadcast([P, 2, D]), op=ALU.subtract,
-            )
-            d_t[q] = d
-
-        def weigh(q):
+        def norm(q):
             rs = stat.tile([P, 2], F32, name="rs")
             nc.vector.reciprocal(out=rs[:], in_=ssum_t[q][:])
-            u = work.tile([P, 2, D], BF16, name="u")
             for a in range(2):
-                nc.vector.scalar_tensor_tensor(
-                    out=u[:, a, :], in0=d_t[q][:, a, :], scalar=rs[:, a:a + 1], in1=e_t[q][:, a, :],
-                    op0=ALU.mult, op1=ALU.mult,
-                )
-            xt = ps_xt.tile([P, 2, KT, P], BF16, name="xt")
-            for a in range(2):
-                for t in range(KT):
-                    nc.tensor.transpose(xt[:, a, t, :], u[:, a, t * P:(t + 1) * P], ident_bf[:])
-            xt_t[q] = xt
+                if norm_on_vector(q, a):
+                    nc.vector.tensor_scalar(out=e_t[q][:, a, :], in0=e_t[q][:, a, :], scalar1=rs[:, a:a + 1],
+                                            scalar2=None, op0=ALU.mult)
+                else:
+                    nc.scalar.activation(out=e_t[q][:, a, :], in_=e_t[q][:, a, :], func=ACT.Copy,
+                                         scale=rs[:, a:a + 1])
 
-        def regroup(q):
+        def smtr(q):
+            sms = []
+            for a in range(2):
+                sm = ps_sm.tile([P, KT, P], F32, name="sm")
+                for t in range(KT):
+                    nc.tensor.transpose(sm[:, t, :], e_t[q][:, a, t * P:(t + 1) * P], ident_f[:])
+                sms.append(sm)
+            sm_t[q] = sms
+
+        def mult(q):
+            h = q // 2
             grp = work.tile([P, 2, P, KT], BF16, name="grp", align_bytes=64)
-            nc.scalar.copy(out=grp[:], in_=xt_t[q][:].rearrange("p a t r -> p a r t"))
+            for a in range(2):
+                c0 = (2 * (q % 2) + a) * P
+                nc.vector.tensor_tensor(
+                    out=grp[:, a, :, :],
+                    in0=dt_t[h][:, :, c0:c0 + P].rearrange("p t r -> p r t"),
+                    in1=sm_t[q][a][:].rearrange("p t r -> p r t"),
+                    op=ALU.mult,
+                )
             grp_t[q] = grp
 
         def quant(q):
@@ -202,44 +234,48 @@ def tile_crosschannelinterp_t_kernel(tc, x, kernel, out):
             nc.scalar.activation(out=ob[:, :, D:2 * D], in_=xb[b][:, j0:j0 + 2, D:2 * D], func=ACT.Exp)
             ob_t[q] = ob
 
-        def post(q):
+        def smooth(q):
+            b = q // 4
+            for a in range(2):
+                nc.vector.tensor_tensor(out=ob_t[q][:, a, 0:D], in0=pp_t[q][a][:], in1=mean_sb[b][:],
+                                        op=ALU.add)
+
+        def ytrans(q):
             b, j0 = q // 4, 2 * (q % 4)
             ob = ob_t[q]
-            for a in range(2):
-                nc.vector.tensor_tensor(out=ob[:, a, 0:D], in0=pp_t[q][a][:], in1=mean_sb[b][:], op=ALU.add)
             nc.vector.tensor_tensor(out=ob[:, :, 2 * D:3 * D], in0=xb[b][:, j0:j0 + 2, 2 * D:3 * D],
                                     in1=ob[:, :, 0:D], op=ALU.subtract)
             nc.sync.dma_start(out=ov[b][:, j0:j0 + 2, :], in_=ob[:])
 
-        mean_mm(0)
-        mean_rep(0)
-        mean_tr(0)
-        rowmax(0)
-        expo(0, 0)
-        expo(0, 1)
-        mean_copy(0)
-        for s in range(NPAIR + 2):
-            nxt = s // 4 + 1
-            if 0 <= s - 2 < NPAIR:
-                post(s - 2)
-            if s % 4 == 2 and nxt < NB:
-                mean_rep(nxt)
-                mean_tr(nxt)
-            if s + 1 < NPAIR:
-                expo(s + 1, 0)
-            if s + 2 < NPAIR and s % 2 == 0:
-                rowmax((s + 2) // 2)
-            if s < NPAIR:
-                centre(s)
-            if 0 <= s - 1 < NPAIR:
-                regroup(s - 1)
-                quant(s - 1)
-                intensity(s - 1)
-            if s + 1 < NPAIR:
-                expo(s + 1, 1)
-            if s % 4 == 2 and nxt < NB:
-                mean_copy(nxt)
-            if s < NPAIR:
-                weigh(s)
-            if s % 4 == 1 and nxt < NB:
-                mean_mm(nxt)
+        def live(q):
+            return 0 <= q < NPAIR
+
+        for s in range(-3, NPAIR + 1):
+            if live(s + 1):
+                norm(s + 1)
+            if live(s):
+                mult(s)
+            if live(s + 1):
+                smtr(s + 1)
+            if live(s - 1):
+                smooth(s - 1)
+            if live(s):
+                quant(s)
+            if live(s - 1):
+                ytrans(s - 1)
+            if s % 2 == 0 and 0 <= (s + 2) // 2 < NQUAD:
+                centre((s + 2) // 2, 0)
+            if s % 2 == 1 and 0 <= (s + 1) // 2 < NQUAD:
+                centre((s + 1) // 2, 1)
+            if live(s + 2):
+                expo(s + 2)
+            if live(s):
+                intensity(s)
+            if s % 4 == 2 and (s + 2) // 4 < NB:
+                mean_bc((s + 2) // 4)
+            if s % 2 == 1 and (s + 3) // 2 < NQUAD:
+                h = (s + 3) // 2
+                if h % 2 == 0:
+                    mean_mm(h // 2)
+                ytr(h)
+                rowmax(h)

@@ -24,7 +24,7 @@ FLOPS = 2 * NB * T * D * D
 
 
 def norm_on_vector(q, a):
-    return a == 0 and q % 2 == 0
+    return q < 2 or (a == 0 and q % 2 == 0)
 
 
 def tile_crosschannelinterp_t_kernel(tc, x, kernel, out):
@@ -40,42 +40,55 @@ def tile_crosschannelinterp_t_kernel(tc, x, kernel, out):
         ps_yt = ctx.enter_context(tc.psum_pool(name="ps_yt", bufs=2))
         ps_sm = ctx.enter_context(tc.psum_pool(name="ps_sm", bufs=3))
         ps_p = ctx.enter_context(tc.psum_pool(name="ps_p", bufs=2))
+        ctx.enter_context(tc.manual_schedule())
 
         xv = [x[b].rearrange("(p j) c -> p j c", j=J) for b in range(NB)]
         ov = [out[b].rearrange("(p j) c -> p j c", j=J) for b in range(NB)]
 
         kraw = const.tile([P, KT, D], BF16, name="kraw")
+        xb = [xpool.tile([P, J, 3 * D], BF16, name="x%d" % b) for b in range(NB)]
+
+        def load(b, j0, j1, c0, c1):
+            nc.sync.dma_start(out=xb[b][:, j0:j1, c0:c1], in_=xv[b][:, j0:j1, c0:c1])
+
+        load(0, 0, 4, D, 2 * D)
+        load(0, 0, 4, 0, D)
+        load(0, 4, 8, 0, D)
+        load(0, 4, 8, D, 2 * D)
         nc.sync.dma_start(
             out=kraw[:].rearrange("q (u e) n -> q u e n", u=2),
             in_=kernel.rearrange("(u q e) n -> q u e n", u=2, e=2),
         )
-        xb = [xpool.tile([P, J, 3 * D], BF16, name="x%d" % b) for b in range(NB)]
-        nc.sync.dma_start(out=xb[0][:, :, 0:D], in_=xv[0][:, :, 0:D])
-        nc.sync.dma_start(out=xb[0][:, 0:4, D:2 * D], in_=xv[0][:, 0:4, D:2 * D])
-        nc.sync.dma_start(out=xb[0][:, 4:8, D:2 * D], in_=xv[0][:, 4:8, D:2 * D])
-        nc.sync.dma_start(out=xb[0][:, :, 2 * D:3 * D], in_=xv[0][:, :, 2 * D:3 * D])
-        for b in range(1, NB):
-            nc.sync.dma_start(out=xb[b][:, 0:4, :], in_=xv[b][:, 0:4, :])
-            nc.sync.dma_start(out=xb[b][:, 4:8, :], in_=xv[b][:, 4:8, :])
+        load(1, 0, 4, 0, 3 * D)
+        load(0, 0, 8, 2 * D, 3 * D)
+        load(1, 4, 8, 0, 3 * D)
+        for b in range(2, NB):
+            load(b, 0, 4, 0, 3 * D)
+            load(b, 4, 8, 0, 3 * D)
 
         ident_f = const.tile([P, P], F32, name="ident_f")
         make_identity(nc, ident_f[:])
         ones = const.tile([P, ONES_N], BF16, name="ones")
-        nc.vector.memset(ones[:], 1.0)
+        nc.vector.memset(ones[:], 1.0 / T)
 
         kgrp = const.tile([P, D, KT], BF16, name="kgrp", align_bytes=64)
-        nc.vector.tensor_copy(out=kgrp[:], in_=kraw[:].rearrange("p t n -> p n t"))
         kcodes = const.tile([P, D], U32, name="kcodes", align_bytes=64)
         kscl = const.tile([P, D], U8, name="kscl", align_bytes=64)
-        nc.vector.quantize_mx(
-            out=kcodes[:].bitcast(FP8X4),
-            scales=kscl[:],
-            in_=kgrp[:].rearrange("p n t -> p (n t)"),
-        )
+
+        def kprep():
+            nc.vector.tensor_copy(out=kgrp[:], in_=kraw[:].rearrange("p t n -> p n t"))
+            nc.vector.quantize_mx(
+                out=kcodes[:].bitcast(FP8X4),
+                scales=kscl[:],
+                in_=kgrp[:].rearrange("p n t -> p (n t)"),
+            )
 
         msum_t = {}
         negmean = {}
+        rep_t = {}
+        mbc_t = {}
         mean_sb = {}
+        tree_t = {}
         negmax = {}
         yt_t = {}
         dt_t = {}
@@ -84,82 +97,96 @@ def tile_crosschannelinterp_t_kernel(tc, x, kernel, out):
         rs_t = {}
         sm_t = {}
         grp_t = {}
+        cod_t = {}
         ob_t = {}
         pp_t = {}
 
-        def mean_mm(b):
-            msum = ps_mean.tile([P, KT, ONES_N], F32, name="msum", tag="mean")
+        def mean_mm(b, half):
+            if half == 0:
+                msum_t[b] = ps_mean.tile([P, 2, KT, ONES_N], F32, name="msum", tag="mean")
             for t in range(KT):
-                for j in range(J):
+                for j in range(4 * half, 4 * half + 4):
                     ysel = xb[b][:, j, 0:D].rearrange("p (u q e) -> p u e q", u=2, e=2)
                     nc.tensor.matmul(
-                        out=msum[:, t, :],
+                        out=msum_t[b][:, half, t, :],
                         lhsT=ysel[:, t // 2, t % 2, :],
                         rhs=ones[:],
-                        start=(j == 0),
-                        stop=(j == J - 1),
+                        start=(j == 4 * half),
+                        stop=(j == 4 * half + 3),
                     )
-            msum_t[b] = msum
-            nm = stat.tile([P, KT, 1], F32, name="negmean")
-            nc.vector.tensor_scalar(out=nm[:], in0=msum[:, :, 0:1], scalar1=-1.0 / T, scalar2=None,
-                                    op0=ALU.mult)
+
+        def neg_mean(b):
+            nm = stat.tile([P, KT], F32, name="negmean")
+            nc.vector.tensor_reduce(out=nm[:], in_=msum_t[b][:, :, :, 0].rearrange("p h t -> p t h"),
+                                    axis=AX.X, op=ALU.add, negate=True)
             negmean[b] = nm
 
-        def mean_bc(b):
+        def mean_rep(b):
             rep = work.tile([P, KT, P], F32, name="rep")
-            nc.vector.tensor_scalar(
+            nc.gpsimd.tensor_scalar(
                 out=rep[:],
-                in0=msum_t[b][:, :, 0:1].to_broadcast([P, KT, P]),
-                scalar1=1.0 / T,
-                scalar2=None,
+                in0=negmean[b][:].unsqueeze(2).to_broadcast([P, KT, P]),
+                scalar1=-1.0,
+                scalar2=0.0,
                 op0=ALU.mult,
+                op1=ALU.add,
             )
+            rep_t[b] = rep
+
+        def mean_tr(b):
             mbc = ps_mean.tile([P, KT, P], F32, name="mbc", tag="mean")
             for t in range(KT):
-                nc.tensor.transpose(mbc[:, t, :], rep[:, t, :], ident_f[:])
+                nc.tensor.transpose(mbc[:, t, :], rep_t[b][:, t, :], ident_f[:])
+            mbc_t[b] = mbc
+
+        def mean_copy(b):
             msb = work.tile([P, D], F32, name="msb")
             nc.scalar.copy(
                 out=msb[:].rearrange("p (u q e) -> p u q e", u=2, e=2),
-                in_=mbc[:].rearrange("p (u e) q -> p u q e", u=2),
+                in_=mbc_t[b][:].rearrange("p (u e) q -> p u q e", u=2),
             )
             mean_sb[b] = msb
 
-        def ytr(h):
+        def ytr(h, u):
             b, j0 = h // 2, 4 * (h % 2)
             xw = xb[b][:].bitcast(F32)
-            yts = []
-            for u in range(2):
-                yt = ps_yt.tile([P, 4 * P], F32, name="yt")
-                for a4 in range(4):
-                    nc.tensor.transpose(yt[:, a4 * P:(a4 + 1) * P], xw[:, j0 + a4, u * P:(u + 1) * P],
-                                        ident_f[:])
-                yts.append(yt)
-            yt_t[h] = yts
+            yt = ps_yt.tile([P, 4 * P], F32, name="yt")
+            for a4 in range(4):
+                nc.tensor.transpose(yt[:, a4 * P:(a4 + 1) * P], xw[:, j0 + a4, u * P:(u + 1) * P],
+                                    ident_f[:])
+            yt_t[(h, u)] = yt
 
-        def centre(h, u):
+        def centre(h, u, on_vector=False):
             b = h // 2
             if u == 0:
                 dt_t[h] = work.tile([P, KT, 4 * P], F32, name="dT")
-            pairs = yt_t[h][u][:].bitcast(BF16).rearrange("p (r e) -> p r e", e=2)
+            pairs = yt_t[(h, u)][:].bitcast(BF16).rearrange("p (r e) -> p r e", e=2)
             for e in range(2):
                 t = 2 * u + e
-                nc.scalar.activation(out=dt_t[h][:, t, :], in_=pairs[:, :, e], func=ACT.Identity,
-                                     bias=negmean[b][:, t, :], scale=1.0)
+                if on_vector:
+                    nc.vector.tensor_scalar(out=dt_t[h][:, t, :], in0=pairs[:, :, e],
+                                            scalar1=negmean[b][:, t:t + 1], scalar2=None, op0=ALU.add)
+                else:
+                    nc.scalar.activation(out=dt_t[h][:, t, :], in_=pairs[:, :, e], func=ACT.Identity,
+                                         bias=negmean[b][:, t:t + 1], scale=1.0)
 
-        def rowmax(h):
+        def tree(h, level):
             b, j0 = h // 2, 4 * (h % 2)
-            t1 = work.tile([P, 4, 256], BF16, name="t1")
-            nc.vector.tensor_tensor(out=t1[:], in0=xb[b][:, j0:j0 + 4, D:D + 256],
-                                    in1=xb[b][:, j0:j0 + 4, D + 256:2 * D], op=ALU.max)
-            t2 = work.tile([P, 4, 128], BF16, name="t2")
-            nc.vector.tensor_tensor(out=t2[:], in0=t1[:, :, 0:128], in1=t1[:, :, 128:256], op=ALU.max)
-            t3 = work.tile([P, 4, 64], BF16, name="t3")
-            nc.vector.tensor_tensor(out=t3[:], in0=t2[:, :, 0:64], in1=t2[:, :, 64:128], op=ALU.max)
-            t4 = work.tile([P, 4, 32], BF16, name="t4")
-            nc.vector.tensor_tensor(out=t4[:], in0=t3[:, :, 0:32], in1=t3[:, :, 32:64], op=ALU.max)
-            nm = stat.tile([P, 4], F32, name="nm")
-            nc.vector.tensor_reduce(out=nm[:], in_=t4[:], axis=AX.X, op=ALU.max, negate=True)
-            negmax[h] = nm
+            if level == 0:
+                t1 = work.tile([P, 4, 256], BF16, name="t1")
+                nc.vector.tensor_tensor(out=t1[:], in0=xb[b][:, j0:j0 + 4, D:D + 256],
+                                        in1=xb[b][:, j0:j0 + 4, D + 256:2 * D], op=ALU.max)
+                tree_t[h] = t1
+            elif level < 4:
+                w = 256 >> level
+                src = tree_t[h]
+                dst = work.tile([P, 4, w], BF16, name="t%d" % (level + 1))
+                nc.vector.tensor_tensor(out=dst[:], in0=src[:, :, 0:w], in1=src[:, :, w:2 * w], op=ALU.max)
+                tree_t[h] = dst
+            else:
+                nm = stat.tile([P, 4], F32, name="nm")
+                nc.vector.tensor_reduce(out=nm[:], in_=tree_t[h][:], axis=AX.X, op=ALU.max, negate=True)
+                negmax[h] = nm
 
         def expo(q):
             b, j0 = q // 4, 2 * (q % 4)
@@ -174,38 +201,36 @@ def tile_crosschannelinterp_t_kernel(tc, x, kernel, out):
                     bias=negmax[q // 2][:, col:col + 1], scale=1.0, accum_out=ssum_t[q][:, a:a + 1],
                 )
 
-        def norm(q):
+        def recip(q):
             rs = stat.tile([P, 2], F32, name="rs")
             nc.vector.reciprocal(out=rs[:], in_=ssum_t[q][:])
-            for a in range(2):
-                if norm_on_vector(q, a):
-                    nc.vector.tensor_scalar(out=e_t[q][:, a, :], in0=e_t[q][:, a, :], scalar1=rs[:, a:a + 1],
-                                            scalar2=None, op0=ALU.mult)
-                else:
-                    nc.scalar.activation(out=e_t[q][:, a, :], in_=e_t[q][:, a, :], func=ACT.Copy,
-                                         scale=rs[:, a:a + 1])
+            rs_t[q] = rs
 
-        def smtr(q):
-            sms = []
-            for a in range(2):
-                sm = ps_sm.tile([P, KT, P], F32, name="sm")
-                for t in range(KT):
-                    nc.tensor.transpose(sm[:, t, :], e_t[q][:, a, t * P:(t + 1) * P], ident_f[:])
-                sms.append(sm)
-            sm_t[q] = sms
+        def norm(q, a):
+            if norm_on_vector(q, a):
+                nc.vector.tensor_scalar(out=e_t[q][:, a, :], in0=e_t[q][:, a, :], scalar1=rs_t[q][:, a:a + 1],
+                                        scalar2=None, op0=ALU.mult)
+            else:
+                nc.scalar.activation(out=e_t[q][:, a, :], in_=e_t[q][:, a, :], func=ACT.Copy,
+                                     scale=rs_t[q][:, a:a + 1])
 
-        def mult(q):
+        def smtr(q, a):
+            sm = ps_sm.tile([P, KT, P], F32, name="sm")
+            for t in range(KT):
+                nc.tensor.transpose(sm[:, t, :], e_t[q][:, a, t * P:(t + 1) * P], ident_f[:])
+            sm_t[(q, a)] = sm
+
+        def mult(q, a):
             h = q // 2
-            grp = work.tile([P, 2, P, KT], BF16, name="grp", align_bytes=64)
-            for a in range(2):
-                c0 = (2 * (q % 2) + a) * P
-                nc.vector.tensor_tensor(
-                    out=grp[:, a, :, :],
-                    in0=dt_t[h][:, :, c0:c0 + P].rearrange("p t r -> p r t"),
-                    in1=sm_t[q][a][:].rearrange("p t r -> p r t"),
-                    op=ALU.mult,
-                )
-            grp_t[q] = grp
+            if a == 0:
+                grp_t[q] = work.tile([P, 2, P, KT], BF16, name="grp", align_bytes=64)
+            c0 = (2 * (q % 2) + a) * P
+            nc.vector.tensor_tensor(
+                out=grp_t[q][:, a, :, :],
+                in0=dt_t[h][:, :, c0:c0 + P].rearrange("p t r -> p r t"),
+                in1=sm_t[(q, a)][:].rearrange("p t r -> p r t"),
+                op=ALU.mult,
+            )
 
         def quant(q):
             codes = work.tile([P, 2 * P], U32, name="codes", align_bytes=64)
@@ -214,7 +239,10 @@ def tile_crosschannelinterp_t_kernel(tc, x, kernel, out):
                 out=codes[:].bitcast(FP8X4), scales=scl[:],
                 in_=grp_t[q][:].rearrange("p a r t -> p (a r t)"),
             )
-            pps = []
+            cod_t[q] = (codes, scl)
+
+        def mxmm(q):
+            codes, scl = cod_t[q]
             for a in range(2):
                 pp = ps_p.tile([P, D], F32, name="pp")
                 nc.tensor.matmul_mx(
@@ -225,8 +253,7 @@ def tile_crosschannelinterp_t_kernel(tc, x, kernel, out):
                     rhs_scale=kscl[:],
                     start=True, stop=True,
                 )
-                pps.append(pp)
-            pp_t[q] = pps
+                pp_t[(q, a)] = pp
 
         def intensity(q):
             b, j0 = q // 4, 2 * (q % 4)
@@ -234,48 +261,129 @@ def tile_crosschannelinterp_t_kernel(tc, x, kernel, out):
             nc.scalar.activation(out=ob[:, :, D:2 * D], in_=xb[b][:, j0:j0 + 2, D:2 * D], func=ACT.Exp)
             ob_t[q] = ob
 
-        def smooth(q):
-            b = q // 4
-            for a in range(2):
-                nc.vector.tensor_tensor(out=ob_t[q][:, a, 0:D], in0=pp_t[q][a][:], in1=mean_sb[b][:],
-                                        op=ALU.add)
+        def smooth(q, a):
+            nc.vector.tensor_tensor(out=ob_t[q][:, a, 0:D], in0=pp_t[(q, a)][:], in1=mean_sb[q // 4][:],
+                                    op=ALU.add)
 
-        def ytrans(q):
+        def ytrans(q, a):
             b, j0 = q // 4, 2 * (q % 4)
             ob = ob_t[q]
-            nc.vector.tensor_tensor(out=ob[:, :, 2 * D:3 * D], in0=xb[b][:, j0:j0 + 2, 2 * D:3 * D],
-                                    in1=ob[:, :, 0:D], op=ALU.subtract)
-            nc.sync.dma_start(out=ov[b][:, j0:j0 + 2, :], in_=ob[:])
+            nc.vector.tensor_tensor(out=ob[:, a, 2 * D:3 * D], in0=xb[b][:, j0 + a, 2 * D:3 * D],
+                                    in1=ob[:, a, 0:D], op=ALU.subtract)
+
+        def store(q, a0, a1, c0, c1):
+            b, j0 = q // 4, 2 * (q % 4)
+            nc.sync.dma_start(out=ov[b][:, j0 + a0:j0 + a1, c0:c1], in_=ob_t[q][:, a0:a1, c0:c1])
 
         def live(q):
             return 0 <= q < NPAIR
 
-        for s in range(-3, NPAIR + 1):
-            if live(s + 1):
-                norm(s + 1)
+        FINE = (NPAIR - 3, NPAIR - 2, NPAIR - 1)
+
+        intensity(0)
+        for level in range(5):
+            tree(0, level)
+        expo(0)
+        mean_mm(0, 0)
+        mean_mm(0, 1)
+        ytr(0, 0)
+        ytr(0, 1)
+        for level in range(5):
+            tree(1, level)
+        recip(0)
+        norm(0, 0)
+        norm(0, 1)
+        smtr(0, 0)
+        smtr(0, 1)
+        neg_mean(0)
+        mean_rep(0)
+        centre(0, 0)
+        centre(0, 1, on_vector=True)
+        expo(1)
+        mean_tr(0)
+        ytr(1, 0)
+        mean_copy(0)
+
+        for s in range(0, NPAIR + 1):
+            slots = []
+            if s % 2 == 0 and (s + 4) // 2 < NQUAD:
+                slots = [((s + 4) // 2, 0), ((s + 4) // 2, 1), ((s + 4) // 2, 2)]
+            if s % 2 == 1 and (s + 3) // 2 < NQUAD:
+                slots = [((s + 3) // 2, 3), ((s + 3) // 2, 4)]
+            bn = (s + 2) // 4
+            new_mean = s % 4 == 2 and bn < NB
+
             if live(s):
-                mult(s)
+                mult(s, 0)
             if live(s + 1):
-                smtr(s + 1)
+                recip(s + 1)
+                for a in range(2):
+                    if not norm_on_vector(s + 1, a):
+                        norm(s + 1, a)
+            if live(s):
+                mult(s, 1)
+            if live(s + 1):
+                for a in range(2):
+                    if norm_on_vector(s + 1, a):
+                        norm(s + 1, a)
+            if live(s + 1):
+                smtr(s + 1, 0)
+                smtr(s + 1, 1)
+            if len(slots) > 0:
+                tree(slots[0][0], slots[0][1])
+            if new_mean:
+                neg_mean(bn)
+                mean_rep(bn)
             if live(s - 1):
-                smooth(s - 1)
+                smooth(s - 1, 0)
+            if len(slots) > 1:
+                tree(slots[1][0], slots[1][1])
+            if live(s - 1):
+                smooth(s - 1, 1)
+                if s - 1 in FINE:
+                    store(s - 1, 0, 2, 0, D)
+            if s == 0:
+                kprep()
             if live(s):
                 quant(s)
             if live(s - 1):
-                ytrans(s - 1)
-            if s % 2 == 0 and 0 <= (s + 2) // 2 < NQUAD:
+                ytrans(s - 1, 0)
+                if s - 1 in FINE:
+                    store(s - 1, 0, 1, 2 * D, 3 * D)
+            if len(slots) > 2:
+                tree(slots[2][0], slots[2][1])
+            if live(s - 1):
+                ytrans(s - 1, 1)
+                if s - 1 in FINE:
+                    store(s - 1, 1, 2, 2 * D, 3 * D)
+                else:
+                    store(s - 1, 0, 2, 0, 3 * D)
+            if s % 2 == 0 and 1 <= (s + 2) // 2 < NQUAD:
                 centre((s + 2) // 2, 0)
-            if s % 2 == 1 and 0 <= (s + 1) // 2 < NQUAD:
+            if s % 2 == 1 and 1 <= (s + 1) // 2 < NQUAD:
                 centre((s + 1) // 2, 1)
             if live(s + 2):
                 expo(s + 2)
-            if live(s):
+            if 0 < s < FINE[0]:
                 intensity(s)
-            if s % 4 == 2 and (s + 2) // 4 < NB:
-                mean_bc((s + 2) // 4)
-            if s % 2 == 1 and (s + 3) // 2 < NQUAD:
-                h = (s + 3) // 2
-                if h % 2 == 0:
-                    mean_mm(h // 2)
-                ytr(h)
-                rowmax(h)
+            if s == FINE[0]:
+                intensity(s)
+                store(s, 0, 2, D, 2 * D)
+            if s == FINE[1]:
+                for q in FINE[1:]:
+                    intensity(q)
+                    store(q, 0, 2, D, 2 * D)
+            if s % 4 == 3 and (s + 1) // 4 < NB:
+                mean_copy((s + 1) // 4)
+            if s % 2 == 1 and 2 <= (s + 3) // 2 < NQUAD:
+                ytr((s + 3) // 2, 0)
+            if s % 2 == 0 and 1 <= (s + 2) // 2 < NQUAD:
+                ytr((s + 2) // 2, 1)
+            if s % 4 == 0 and (s + 4) // 4 < NB:
+                mean_mm((s + 4) // 4, 0)
+            if s % 4 == 1 and (s + 3) // 4 < NB:
+                mean_mm((s + 3) // 4, 1)
+            if new_mean:
+                mean_tr(bn)
+            if live(s):
+                mxmm(s)

@@ -40,7 +40,6 @@ def tile_crosschannelinterp_t_kernel(tc, x, kernel, out):
         ps_yt = ctx.enter_context(tc.psum_pool(name="ps_yt", bufs=2))
         ps_sm = ctx.enter_context(tc.psum_pool(name="ps_sm", bufs=3))
         ps_p = ctx.enter_context(tc.psum_pool(name="ps_p", bufs=2))
-        ctx.enter_context(tc.manual_schedule())
 
         xv = [x[b].rearrange("(p j) c -> p j c", j=J) for b in range(NB)]
         ov = [out[b].rearrange("(p j) c -> p j c", j=J) for b in range(NB)]
@@ -123,14 +122,8 @@ def tile_crosschannelinterp_t_kernel(tc, x, kernel, out):
 
         def mean_rep(b):
             rep = work.tile([P, KT, P], F32, name="rep")
-            nc.gpsimd.tensor_scalar(
-                out=rep[:],
-                in0=negmean[b][:].unsqueeze(2).to_broadcast([P, KT, P]),
-                scalar1=-1.0,
-                scalar2=0.0,
-                op0=ALU.mult,
-                op1=ALU.add,
-            )
+            nc.scalar.activation(out=rep[:], in_=negmean[b][:].unsqueeze(2).to_broadcast([P, KT, P]),
+                                 func=ACT.Copy, scale=-1.0)
             rep_t[b] = rep
 
         def mean_tr(b):
@@ -265,11 +258,11 @@ def tile_crosschannelinterp_t_kernel(tc, x, kernel, out):
             nc.vector.tensor_tensor(out=ob_t[q][:, a, 0:D], in0=pp_t[(q, a)][:], in1=mean_sb[q // 4][:],
                                     op=ALU.add)
 
-        def ytrans(q, a):
+        def ytrans(q, a0, a1):
             b, j0 = q // 4, 2 * (q % 4)
             ob = ob_t[q]
-            nc.vector.tensor_tensor(out=ob[:, a, 2 * D:3 * D], in0=xb[b][:, j0 + a, 2 * D:3 * D],
-                                    in1=ob[:, a, 0:D], op=ALU.subtract)
+            nc.vector.tensor_tensor(out=ob[:, a0:a1, 2 * D:3 * D], in0=xb[b][:, j0 + a0:j0 + a1, 2 * D:3 * D],
+                                    in1=ob[:, a0:a1, 0:D], op=ALU.subtract)
 
         def store(q, a0, a1, c0, c1):
             b, j0 = q // 4, 2 * (q % 4)
@@ -346,17 +339,17 @@ def tile_crosschannelinterp_t_kernel(tc, x, kernel, out):
                 kprep()
             if live(s):
                 quant(s)
-            if live(s - 1):
-                ytrans(s - 1, 0)
-                if s - 1 in FINE:
-                    store(s - 1, 0, 1, 2 * D, 3 * D)
+            if s - 1 in FINE:
+                ytrans(s - 1, 0, 1)
+                store(s - 1, 0, 1, 2 * D, 3 * D)
             if len(slots) > 2:
                 tree(slots[2][0], slots[2][1])
             if live(s - 1):
-                ytrans(s - 1, 1)
                 if s - 1 in FINE:
+                    ytrans(s - 1, 1, 2)
                     store(s - 1, 1, 2, 2 * D, 3 * D)
                 else:
+                    ytrans(s - 1, 0, 2)
                     store(s - 1, 0, 2, 0, 3 * D)
             if s % 2 == 0 and 1 <= (s + 2) // 2 < NQUAD:
                 centre((s + 2) // 2, 0)

@@ -261,8 +261,9 @@ def tile_crosschannelinterp_t_kernel(tc, x, kernel, out):
         def ytrans(q, a0, a1):
             b, j0 = q // 4, 2 * (q % 4)
             ob = ob_t[q]
-            nc.vector.tensor_tensor(out=ob[:, a0:a1, 2 * D:3 * D], in0=xb[b][:, j0 + a0:j0 + a1, 2 * D:3 * D],
-                                    in1=ob[:, a0:a1, 0:D], op=ALU.subtract)
+            eng = nc.vector if q == NPAIR - 1 else nc.gpsimd
+            eng.tensor_tensor(out=ob[:, a0:a1, 2 * D:3 * D], in0=xb[b][:, j0 + a0:j0 + a1, 2 * D:3 * D],
+                              in1=ob[:, a0:a1, 0:D], op=ALU.subtract)
 
         def store(q, a0, a1, c0, c1):
             b, j0 = q // 4, 2 * (q % 4)
@@ -349,7 +350,8 @@ def tile_crosschannelinterp_t_kernel(tc, x, kernel, out):
                     ytrans(s - 1, 1, 2)
                     store(s - 1, 1, 2, 2 * D, 3 * D)
                 else:
-                    ytrans(s - 1, 0, 2)
+                    ytrans(s - 1, 0, 1)
+                    ytrans(s - 1, 1, 2)
                     store(s - 1, 0, 2, 0, 3 * D)
             if s % 2 == 0 and 1 <= (s + 2) // 2 < NQUAD:
                 centre((s + 2) // 2, 0)

@@ -219,9 +219,9 @@ def tile_crosschannelinterp_t_kernel(tc, x, kernel, out):
                 grp_t[q] = work.tile([P, 2, P, KT], BF16, name="grp", align_bytes=64)
             c0 = (2 * (q % 2) + a) * P
             nc.vector.tensor_tensor(
-                out=grp_t[q][:, a, :, :],
-                in0=dt_t[h][:, :, c0:c0 + P].rearrange("p t r -> p r t"),
-                in1=sm_t[(q, a)][:].rearrange("p t r -> p r t"),
+                out=grp_t[q][:, a, :, :].rearrange("p (c i) t -> p c t i", i=4),
+                in0=dt_t[h][:, :, c0:c0 + P].rearrange("p t (c i) -> p c t i", i=4),
+                in1=sm_t[(q, a)][:].rearrange("p t (c i) -> p c t i", i=4),
                 op=ALU.mult,
             )
 
@@ -261,9 +261,8 @@ def tile_crosschannelinterp_t_kernel(tc, x, kernel, out):
         def ytrans(q, a0, a1):
             b, j0 = q // 4, 2 * (q % 4)
             ob = ob_t[q]
-            eng = nc.vector if q == NPAIR - 1 else nc.gpsimd
-            eng.tensor_tensor(out=ob[:, a0:a1, 2 * D:3 * D], in0=xb[b][:, j0 + a0:j0 + a1, 2 * D:3 * D],
-                              in1=ob[:, a0:a1, 0:D], op=ALU.subtract)
+            nc.vector.tensor_tensor(out=ob[:, a0:a1, 2 * D:3 * D], in0=xb[b][:, j0 + a0:j0 + a1, 2 * D:3 * D],
+                                    in1=ob[:, a0:a1, 0:D], op=ALU.subtract)
 
         def store(q, a0, a1, c0, c1):
             b, j0 = q // 4, 2 * (q % 4)
@@ -350,8 +349,7 @@ def tile_crosschannelinterp_t_kernel(tc, x, kernel, out):
                     ytrans(s - 1, 1, 2)
                     store(s - 1, 1, 2, 2 * D, 3 * D)
                 else:
-                    ytrans(s - 1, 0, 1)
-                    ytrans(s - 1, 1, 2)
+                    ytrans(s - 1, 0, 2)
                     store(s - 1, 0, 2, 0, 3 * D)
             if s % 2 == 0 and 1 <= (s + 2) // 2 < NQUAD:
                 centre((s + 2) // 2, 0)

@@ -54,10 +54,7 @@ def tile_crosschannelinterp_t_kernel(tc, x, kernel, out):
         load(0, 0, 4, 0, D)
         load(0, 4, 8, 0, D)
         load(0, 4, 8, D, 2 * D)
-        nc.sync.dma_start(
-            out=kraw[:].rearrange("q (u e) n -> q u e n", u=2),
-            in_=kernel.rearrange("(u q e) n -> q u e n", u=2, e=2),
-        )
+        nc.sync.dma_start(out=kraw[:], in_=kernel.rearrange("(t p) n -> p t n", p=P))
         load(1, 0, 4, 0, 3 * D)
         load(0, 0, 8, 2 * D, 3 * D)
         load(1, 4, 8, 0, 3 * D)
@@ -65,6 +62,8 @@ def tile_crosschannelinterp_t_kernel(tc, x, kernel, out):
             load(b, 0, 4, 0, 3 * D)
             load(b, 4, 8, 0, 3 * D)
 
+        ident_b = const.tile([P, P], BF16, name="ident_b")
+        make_identity(nc, ident_b[:])
         ident_f = const.tile([P, P], F32, name="ident_f")
         make_identity(nc, ident_f[:])
         ones = const.tile([P, ONES_N], BF16, name="ones")
@@ -75,7 +74,8 @@ def tile_crosschannelinterp_t_kernel(tc, x, kernel, out):
         kscl = const.tile([P, D], U8, name="kscl", align_bytes=64)
 
         def kprep():
-            nc.vector.tensor_copy(out=kgrp[:], in_=kraw[:].rearrange("p t n -> p n t"))
+            nc.vector.tensor_copy(out=kgrp[:].rearrange("p (c i) t -> p c t i", i=4),
+                                  in_=kraw[:].rearrange("p t (c i) -> p c t i", i=4))
             nc.vector.quantize_mx(
                 out=kcodes[:].bitcast(FP8X4),
                 scales=kscl[:],
@@ -105,10 +105,9 @@ def tile_crosschannelinterp_t_kernel(tc, x, kernel, out):
                 msum_t[b] = ps_mean.tile([P, 2, KT, ONES_N], F32, name="msum", tag="mean")
             for t in range(KT):
                 for j in range(4 * half, 4 * half + 4):
-                    ysel = xb[b][:, j, 0:D].rearrange("p (u q e) -> p u e q", u=2, e=2)
                     nc.tensor.matmul(
                         out=msum_t[b][:, half, t, :],
-                        lhsT=ysel[:, t // 2, t % 2, :],
+                        lhsT=xb[b][:, j, t * P:(t + 1) * P],
                         rhs=ones[:],
                         start=(j == 4 * half),
                         stop=(j == 4 * half + 3),
@@ -134,33 +133,31 @@ def tile_crosschannelinterp_t_kernel(tc, x, kernel, out):
 
         def mean_copy(b):
             msb = work.tile([P, D], F32, name="msb")
-            nc.scalar.copy(
-                out=msb[:].rearrange("p (u q e) -> p u q e", u=2, e=2),
-                in_=mbc_t[b][:].rearrange("p (u e) q -> p u q e", u=2),
-            )
+            nc.scalar.copy(out=msb[:], in_=mbc_t[b][:].rearrange("p t q -> p (t q)"))
             mean_sb[b] = msb
 
         def ytr(h, u):
             b, j0 = h // 2, 4 * (h % 2)
-            xw = xb[b][:].bitcast(F32)
-            yt = ps_yt.tile([P, 4 * P], F32, name="yt")
-            for a4 in range(4):
-                nc.tensor.transpose(yt[:, a4 * P:(a4 + 1) * P], xw[:, j0 + a4, u * P:(u + 1) * P],
-                                    ident_f[:])
+            yt = ps_yt.tile([P, 2, 4 * P], BF16, name="yt")
+            for e in range(2):
+                t = 2 * u + e
+                for a4 in range(4):
+                    nc.tensor.transpose(yt[:, e, a4 * P:(a4 + 1) * P], xb[b][:, j0 + a4, t * P:(t + 1) * P],
+                                        ident_b[:])
             yt_t[(h, u)] = yt
 
         def centre(h, u, on_vector=False):
             b = h // 2
             if u == 0:
                 dt_t[h] = work.tile([P, KT, 4 * P], F32, name="dT")
-            pairs = yt_t[(h, u)][:].bitcast(BF16).rearrange("p (r e) -> p r e", e=2)
+            halves = yt_t[(h, u)]
             for e in range(2):
                 t = 2 * u + e
                 if on_vector:
-                    nc.vector.tensor_scalar(out=dt_t[h][:, t, :], in0=pairs[:, :, e],
+                    nc.vector.tensor_scalar(out=dt_t[h][:, t, :], in0=halves[:, e, :],
                                             scalar1=negmean[b][:, t:t + 1], scalar2=None, op0=ALU.add)
                 else:
-                    nc.scalar.activation(out=dt_t[h][:, t, :], in_=pairs[:, :, e], func=ACT.Identity,
+                    nc.scalar.activation(out=dt_t[h][:, t, :], in_=halves[:, e, :], func=ACT.Identity,
                                          bias=negmean[b][:, t:t + 1], scale=1.0)
 
         def tree(h, level):
@@ -188,8 +185,8 @@ def tile_crosschannelinterp_t_kernel(tc, x, kernel, out):
             for a in range(2):
                 col = 2 * (q % 2) + a
                 nc.scalar.activation(
-                    out=e_t[q][:, a, :].rearrange("p (u e q) -> p u e q", u=2, e=2),
-                    in_=xb[b][:, j0 + a, D:2 * D].rearrange("p (u q e) -> p u e q", u=2, e=2),
+                    out=e_t[q][:, a, :],
+                    in_=xb[b][:, j0 + a, D:2 * D],
                     func=ACT.Exp,
                     bias=negmax[q // 2][:, col:col + 1], scale=1.0, accum_out=ssum_t[q][:, a:a + 1],
                 )

from contextlib import ExitStack

import concourse.mybir as mybir
from concourse.masks import make_identity

FP8X4 = mybir.dt.float8_e4m3fn_x4
BF16 = mybir.dt.bfloat16
F32 = mybir.dt.float32
U32 = mybir.dt.uint32
U8 = mybir.dt.uint8
ALU = mybir.AluOpType
ACT = mybir.ActivationFunctionType
AX = mybir.AxisListType

NB, T, D = 4, 1024, 512
P = 128
J = T // P
KT = D // P
NPAIR = NB * J // 2
NQUAD = NB * J // 4
ONES_N = 32

FLOPS = 2 * NB * T * D * D


def norm_on_vector(q, a):
    return q < 2 or (a == 0 and q % 2 == 0)


def tile_crosschannelinterp_t_kernel(tc, x, kernel, out):
    nc = tc.nc
    with ExitStack() as ctx:
        const = ctx.enter_context(tc.tile_pool(name="const", bufs=1))
        xpool = ctx.enter_context(tc.tile_pool(name="xpool", bufs=1))
        opool = ctx.enter_context(tc.tile_pool(name="opool", bufs=5))
        epool = ctx.enter_context(tc.tile_pool(name="epool", bufs=3))
        work = ctx.enter_context(tc.tile_pool(name="work", bufs=2))
        stat = ctx.enter_context(tc.tile_pool(name="stat", bufs=4))
        ps_mean = ctx.enter_context(tc.psum_pool(name="ps_mean", bufs=1))
        ps_yt = ctx.enter_context(tc.psum_pool(name="ps_yt", bufs=2))
        ps_sm = ctx.enter_context(tc.psum_pool(name="ps_sm", bufs=3))
        ps_p = ctx.enter_context(tc.psum_pool(name="ps_p", bufs=2))

        xv = [x[b].rearrange("(p j) c -> p j c", j=J) for b in range(NB)]
        ov = [out[b].rearrange("(p j) c -> p j c", j=J) for b in range(NB)]

        kraw = const.tile([P, KT, D], BF16, name="kraw")
        xb = [xpool.tile([P, J, 3 * D], BF16, name="x%d" % b) for b in range(NB)]

        def load(b, j0, j1, c0, c1):
            nc.sync.dma_start(out=xb[b][:, j0:j1, c0:c1], in_=xv[b][:, j0:j1, c0:c1])

        load(0, 0, 4, D, 2 * D)
        load(0, 0, 4, 0, D)
        load(0, 4, 8, 0, D)
        load(0, 4, 8, D, 2 * D)
        nc.sync.dma_start(out=kraw[:], in_=kernel.rearrange("(t p) n -> p t n", p=P))
        load(1, 0, 4, 0, 3 * D)
        load(0, 0, 8, 2 * D, 3 * D)
        load(1, 4, 8, 0, 3 * D)
        for b in range(2, NB):
            load(b, 0, 4, 0, 3 * D)
            load(b, 4, 8, 0, 3 * D)

        ident_b = const.tile([P, P], BF16, name="ident_b")
        make_identity(nc, ident_b[:])
        ident_f = const.tile([P, P], F32, name="ident_f")
        make_identity(nc, ident_f[:])
        ones = const.tile([P, ONES_N], BF16, name="ones")
        nc.vector.memset(ones[:], 1.0 / T)

        kgrp = const.tile([P, D, KT], BF16, name="kgrp", align_bytes=64)
        kcodes = const.tile([P, D], U32, name="kcodes", align_bytes=64)
        kscl = const.tile([P, D], U8, name="kscl", align_bytes=64)

        def kprep():
            nc.vector.tensor_copy(out=kgrp[:].rearrange("p (c i) t -> p c t i", i=4),
                                  in_=kraw[:].rearrange("p t (c i) -> p c t i", i=4))
            nc.vector.quantize_mx(
                out=kcodes[:].bitcast(FP8X4),
                scales=kscl[:],
                in_=kgrp[:].rearrange("p n t -> p (n t)"),
            )

        msum_t = {}
        negmean = {}
        rep_t = {}
        mbc_t = {}
        mean_sb = {}
        tree_t = {}
        negmax = {}
        yt_t = {}
        dt_t = {}
        e_t = {}
        ssum_t = {}
        rs_t = {}
        sm_t = {}
        grp_t = {}
        cod_t = {}
        ob_t = {}
        pp_t = {}

        def mean_mm(b, half):
            if half == 0:
                msum_t[b] = ps_mean.tile([P, 2, KT, ONES_N], F32, name="msum", tag="mean")
            for t in range(KT):
                for j in range(4 * half, 4 * half + 4):
                    nc.tensor.matmul(
                        out=msum_t[b][:, half, t, :],
                        lhsT=xb[b][:, j, t * P:(t + 1) * P],
                        rhs=ones[:],
                        start=(j == 4 * half),
                        stop=(j == 4 * half + 3),
                    )

        def neg_mean(b):
            nm = stat.tile([P, KT], F32, name="negmean")
            nc.vector.tensor_reduce(out=nm[:], in_=msum_t[b][:, :, :, 0].rearrange("p h t -> p t h"),
                                    axis=AX.X, op=ALU.add, negate=True)
            negmean[b] = nm

        def mean_rep(b):
            rep = work.tile([P, KT, P], F32, name="rep")
            nc.scalar.activation(out=rep[:], in_=negmean[b][:].unsqueeze(2).to_broadcast([P, KT, P]),
                                 func=ACT.Copy, scale=-1.0)
            rep_t[b] = rep

        def mean_tr(b):
            mbc = ps_mean.tile([P, KT, P], F32, name="mbc", tag="mean")
            for t in range(KT):
                nc.tensor.transpose(mbc[:, t, :], rep_t[b][:, t, :], ident_f[:])
            mbc_t[b] = mbc

        def mean_copy(b):
            msb = work.tile([P, D], F32, name="msb")
            nc.scalar.copy(out=msb[:], in_=mbc_t[b][:].rearrange("p t q -> p (t q)"))
            mean_sb[b] = msb

        def ytr(h, u):
            b, j0 = h // 2, 4 * (h % 2)
            yt = ps_yt.tile([P, 2, 4 * P], BF16, name="yt")
            for e in range(2):
                t = 2 * u + e
                for a4 in range(4):
                    nc.tensor.transpose(yt[:, e, a4 * P:(a4 + 1) * P], xb[b][:, j0 + a4, t * P:(t + 1) * P],
                                        ident_b[:])
            yt_t[(h, u)] = yt

        def centre(h, u, on_vector=False):
            b = h // 2
            if u == 0:
                dt_t[h] = work.tile([P, KT, 4 * P], F32, name="dT")
            halves = yt_t[(h, u)]
            for e in range(2):
                t = 2 * u + e
                if on_vector:
                    nc.vector.tensor_scalar(out=dt_t[h][:, t, :], in0=halves[:, e, :],
                                            scalar1=negmean[b][:, t:t + 1], scalar2=None, op0=ALU.add)
                else:
                    nc.scalar.activation(out=dt_t[h][:, t, :], in_=halves[:, e, :], func=ACT.Identity,
                                         bias=negmean[b][:, t:t + 1], scale=1.0)

        def tree(h, level):
            b, j0 = h // 2, 4 * (h % 2)
            if level == 0:
                t1 = work.tile([P, 4, 256], BF16, name="t1")
                nc.vector.tensor_tensor(out=t1[:], in0=xb[b][:, j0:j0 + 4, D:D + 256],
                                        in1=xb[b][:, j0:j0 + 4, D + 256:2 * D], op=ALU.max)
                tree_t[h] = t1
            elif level < 4:
                w = 256 >> level
                src = tree_t[h]
                dst = work.tile([P, 4, w], BF16, name="t%d" % (level + 1))
                nc.vector.tensor_tensor(out=dst[:], in0=src[:, :, 0:w], in1=src[:, :, w:2 * w], op=ALU.max)
                tree_t[h] = dst
            else:
                nm = stat.tile([P, 4], F32, name="nm")
                nc.vector.tensor_reduce(out=nm[:], in_=tree_t[h][:], axis=AX.X, op=ALU.max, negate=True)
                negmax[h] = nm

        def expo(q):
            b, j0 = q // 4, 2 * (q % 4)
            e_t[q] = epool.tile([P, 2, D], F32, name="e")
            ssum_t[q] = stat.tile([P, 2], F32, name="ssum")
            for a in range(2):
                col = 2 * (q % 2) + a
                nc.scalar.activation(
                    out=e_t[q][:, a, :],
                    in_=xb[b][:, j0 + a, D:2 * D],
                    func=ACT.Exp,
                    bias=negmax[q // 2][:, col:col + 1], scale=1.0, accum_out=ssum_t[q][:, a:a + 1],
                )

        def recip(q):
            rs = stat.tile([P, 2], F32, name="rs")
            nc.vector.reciprocal(out=rs[:], in_=ssum_t[q][:])
            rs_t[q] = rs

        def norm(q, a):
            if norm_on_vector(q, a):
                nc.vector.tensor_scalar(out=e_t[q][:, a, :], in0=e_t[q][:, a, :], scalar1=rs_t[q][:, a:a + 1],
                                        scalar2=None, op0=ALU.mult)
            else:
                nc.scalar.activation(out=e_t[q][:, a, :], in_=e_t[q][:, a, :], func=ACT.Copy,
                                     scale=rs_t[q][:, a:a + 1])

        def smtr(q, a):
            sm = ps_sm.tile([P, KT, P], F32, name="sm")
            for t in range(KT):
                nc.tensor.transpose(sm[:, t, :], e_t[q][:, a, t * P:(t + 1) * P], ident_f[:])
            sm_t[(q, a)] = sm

        def mult(q, a):
            h = q // 2
            if a == 0:
                grp_t[q] = work.tile([P, 2, P, KT], BF16, name="grp", align_bytes=64)
            c0 = (2 * (q % 2) + a) * P
            nc.vector.tensor_tensor(
                out=grp_t[q][:, a, :, :].rearrange("p (c i) t -> p c t i", i=4),
                in0=dt_t[h][:, :, c0:c0 + P].rearrange("p t (c i) -> p c t i", i=4),
                in1=sm_t[(q, a)][:].rearrange("p t (c i) -> p c t i", i=4),
                op=ALU.mult,
            )

        def quant(q):
            codes = work.tile([P, 2 * P], U32, name="codes", align_bytes=64)
            scl = work.tile([P, 2 * P], U8, name="scl", align_bytes=64)
            nc.vector.quantize_mx(
                out=codes[:].bitcast(FP8X4), scales=scl[:],
                in_=grp_t[q][:].rearrange("p a r t -> p (a r t)"),
            )
            cod_t[q] = (codes, scl)

        def mxmm(q):
            codes, scl = cod_t[q]
            for a in range(2):
                pp = ps_p.tile([P, D], F32, name="pp")
                nc.tensor.matmul_mx(
                    out=pp[:],
                    lhsT=codes[:, a * P:(a + 1) * P].bitcast(FP8X4),
                    lhsT_scale=scl[:, a * P:(a + 1) * P],
                    rhs=kcodes[:].bitcast(FP8X4),
                    rhs_scale=kscl[:],
                    start=True, stop=True,
                )
                pp_t[(q, a)] = pp

        def intensity(q):
            b, j0 = q // 4, 2 * (q % 4)
            ob = opool.tile([P, 2, 3 * D], F32, name="ob")
            nc.scalar.activation(out=ob[:, :, D:2 * D], in_=xb[b][:, j0:j0 + 2, D:2 * D], func=ACT.Exp)
            ob_t[q] = ob

        def smooth(q, a):
            nc.vector.tensor_tensor(out=ob_t[q][:, a, 0:D], in0=pp_t[(q, a)][:], in1=mean_sb[q // 4][:],
                                    op=ALU.add)

        def ytrans(q, a0, a1):
            b, j0 = q // 4, 2 * (q % 4)
            ob = ob_t[q]
            nc.vector.tensor_tensor(out=ob[:, a0:a1, 2 * D:3 * D], in0=xb[b][:, j0 + a0:j0 + a1, 2 * D:3 * D],
                                    in1=ob[:, a0:a1, 0:D], op=ALU.subtract)

        def store(q, a0, a1, c0, c1):
            b, j0 = q // 4, 2 * (q % 4)
            nc.sync.dma_start(out=ov[b][:, j0 + a0:j0 + a1, c0:c1], in_=ob_t[q][:, a0:a1, c0:c1])

        def live(q):
            return 0 <= q < NPAIR

        FINE = (NPAIR - 3, NPAIR - 2, NPAIR - 1)

        intensity(0)
        for level in range(5):
            tree(0, level)
        expo(0)
        mean_mm(0, 0)
        mean_mm(0, 1)
        ytr(0, 0)
        ytr(0, 1)
        for level in range(5):
            tree(1, level)
        recip(0)
        norm(0, 0)
        norm(0, 1)
        smtr(0, 0)
        smtr(0, 1)
        neg_mean(0)
        mean_rep(0)
        centre(0, 0)
        centre(0, 1, on_vector=True)
        expo(1)
        mean_tr(0)
        ytr(1, 0)
        mean_copy(0)

        for s in range(0, NPAIR + 1):
            slots = []
            if s % 2 == 0 and (s + 4) // 2 < NQUAD:
                slots = [((s + 4) // 2, 0), ((s + 4) // 2, 1), ((s + 4) // 2, 2)]
            if s % 2 == 1 and (s + 3) // 2 < NQUAD:
                slots = [((s + 3) // 2, 3), ((s + 3) // 2, 4)]
            bn = (s + 2) // 4
            new_mean = s % 4 == 2 and bn < NB

            if live(s):
                mult(s, 0)
            if live(s + 1):
                recip(s + 1)
                for a in range(2):
                    if not norm_on_vector(s + 1, a):
                        norm(s + 1, a)
            if live(s):
                mult(s, 1)
            if live(s + 1):
                for a in range(2):
                    if norm_on_vector(s + 1, a):
                        norm(s + 1, a)
            if live(s + 1):
                smtr(s + 1, 0)
                smtr(s + 1, 1)
            if len(slots) > 0:
                tree(slots[0][0], slots[0][1])
            if new_mean:
                neg_mean(bn)
                mean_rep(bn)
            if live(s - 1):
                smooth(s - 1, 0)
            if len(slots) > 1:
                tree(slots[1][0], slots[1][1])
            if live(s - 1):
                smooth(s - 1, 1)
                if s - 1 in FINE:
                    store(s - 1, 0, 2, 0, D)
            if s == 0:
                kprep()
            if live(s):
                quant(s)
            if s - 1 in FINE:
                ytrans(s - 1, 0, 1)
                store(s - 1, 0, 1, 2 * D, 3 * D)
            if len(slots) > 2:
                tree(slots[2][0], slots[2][1])
            if live(s - 1):
                if s - 1 in FINE:
                    ytrans(s - 1, 1, 2)
                    store(s - 1, 1, 2, 2 * D, 3 * D)
                else:
                    ytrans(s - 1, 0, 2)
                    store(s - 1, 0, 2, 0, 3 * D)
            if s % 2 == 0 and 1 <= (s + 2) // 2 < NQUAD:
                centre((s + 2) // 2, 0)
            if s % 2 == 1 and 1 <= (s + 1) // 2 < NQUAD:
                centre((s + 1) // 2, 1)
            if live(s + 2):
                expo(s + 2)
            if 0 < s < FINE[0]:
                intensity(s)
            if s == FINE[0]:
                intensity(s)
                store(s, 0, 2, D, 2 * D)
            if s == FINE[1]:
                for q in FINE[1:]:
                    intensity(q)
                    store(q, 0, 2, D, 2 * D)
            if s % 4 == 3 and (s + 1) // 4 < NB:
                mean_copy((s + 1) // 4)
            if s % 2 == 1 and 2 <= (s + 3) // 2 < NQUAD:
                ytr((s + 3) // 2, 0)
            if s % 2 == 0 and 1 <= (s + 2) // 2 < NQUAD:
                ytr((s + 2) // 2, 1)
            if s % 4 == 0 and (s + 4) // 4 < NB:
                mean_mm((s + 4) // 4, 0)
            if s % 4 == 1 and (s + 3) // 4 < NB:
                mean_mm((s + 3) // 4, 1)
            if new_mean:
                mean_tr(bn)
            if live(s):
                mxmm(s)
